import numpy as np
import ml_dtypes


def mxq(x, axis, fmt="e4m3"):
    dtype, down = {"e4m3": (ml_dtypes.float8_e4m3fn, 7), "e5m2": (ml_dtypes.float8_e5m2, 14)}[fmt]
    v = np.moveaxis(np.asarray(x, np.float32).astype(ml_dtypes.bfloat16).astype(np.float64), axis, -1)
    blocks = v.reshape(v.shape[:-1] + (-1, 32))
    amax = np.abs(blocks).max(-1, keepdims=True)
    byte = np.maximum(np.where(amax > 0, np.frexp(amax)[1] - 1 + 127, 0) - down, 1)
    scale = np.exp2(byte - 127.0)
    codes = (blocks / scale).astype(np.float32).astype(dtype).astype(np.float64)
    return np.moveaxis((codes * scale).reshape(v.shape), -1, axis)


WIDE = False


def mx_kscale(k):
    if not WIDE:
        return np.ones(k)
    levels = np.array([10, -10, 5, -5, 0])
    a = np.random.permutation(np.resize(levels, k // 512 * 4)).reshape(k // 512, 4)
    idx = np.arange(k)
    return np.exp2(a[idx // 512, idx % 128 // 32])


BF16 = ml_dtypes.bfloat16


def bf(x):
    return np.asarray(x, np.float32).astype(BF16)


def f64(x):
    return np.asarray(x).astype(np.float64)


E2M1 = np.array([0.0, 0.5, 1.0, 1.5, 2.0, 3.0, 4.0, 6.0, -0.0, -0.5, -1.0, -1.5, -2.0, -3.0, -4.0, -6.0])


def pack_weight(w, fmt):
    k, n = w.shape
    w = f64(bf(w)).reshape(k // 32, 32, n)
    amax = np.abs(w).max(1)
    if fmt == "e4m3":
        byte = np.frexp(amax)[1] - 1 + 127 - 7
    else:
        mant, ex = np.frexp(amax / 6.0)
        byte = np.where(mant > 0.5, ex, ex - 1) + 127
    byte = np.clip(np.where(amax > 0, byte, 1), 1, 254)
    scaled = (w * np.exp2(127.0 - byte)[:, None, :]).reshape(k, n).astype(np.float32)
    by_word = np.ascontiguousarray(scaled.reshape(k // 512, 128, 4, n).transpose(0, 1, 3, 2))
    if fmt == "e4m3":
        words = by_word.astype(ml_dtypes.float8_e4m3fn).view(np.uint8)
    else:
        c = by_word.astype(ml_dtypes.float4_e2m1fn).view(np.uint8) & 0xF
        words = c[..., 0::2] | (c[..., 1::2] << 4)
    return np.ascontiguousarray(words), np.ascontiguousarray(byte.astype(np.uint8).reshape(k // 512, 16, n))


def unpack_weight(words, scales, fmt):
    g, p, n, _ = words.shape
    if fmt == "e4m3":
        vals = np.ascontiguousarray(words).view(ml_dtypes.float8_e4m3fn).astype(np.float64)
    else:
        nib = np.empty((g, p, n, 4), np.uint8)
        nib[..., 0::2] = words & 0xF
        nib[..., 1::2] = words >> 4
        vals = E2M1[nib]
    vals = vals * np.repeat(np.exp2(scales.astype(np.float64) - 127.0), 8, axis=1)[..., None]
    return vals.transpose(0, 1, 3, 2).reshape(g * 512, n)


B, S, D, NH = 2, 512, 1024, 8
SCALE = np.sqrt(D // NH)
FMT = "e4m3"


def setup_inputs():
    s, t = mx_kscale(D), mx_kscale(D)
    x = bf(np.random.standard_normal((B, S, D)) * s)
    wq = np.random.standard_normal((D, D)) * 0.84 / np.sqrt(D) / s[None, :] * t[:, None]
    wk = np.random.standard_normal((D, D)) * 0.84 / np.sqrt(D) / s[None, :] / t[:, None]
    wq_words, wq_scales = pack_weight(wq.T, FMT)
    wk_words, wk_scales = pack_weight(wk.T, FMT)
    return {"x": x,
            "wq_words": wq_words, "wq_scales": wq_scales,
            "wk_words": wk_words, "wk_scales": wk_scales}


def reference(x, wq_words, wq_scales, wk_words, wk_scales):
    xq = mxq(f64(x), 2, "e4m3")
    q = xq @ unpack_weight(wq_words, wq_scales, FMT)
    k = xq @ unpack_weight(wk_words, wk_scales, FMT)
    sc = (mxq(q, 2, "e4m3") @ mxq(k, 2, "e4m3").transpose(0, 2, 1)) / SCALE
    e = np.exp(sc - sc.max(-1, keepdims=True))
    return e / e.sum(-1, keepdims=True)

@@ -1,0 +1,200 @@
+from contextlib import ExitStack
+import math
+
+import concourse.mybir as mybir
+from concourse.masks import make_identity
+
+F32 = mybir.dt.float32
+BF16 = mybir.dt.bfloat16
+I32 = mybir.dt.int32
+U32 = mybir.dt.uint32
+U8 = mybir.dt.uint8
+FP8X4 = mybir.dt.float8_e4m3fn_x4
+EXP = mybir.ActivationFunctionType.Exp
+MAX = mybir.AluOpType.max
+MULT = mybir.AluOpType.mult
+ROW = mybir.AxisListType.X
+
+P = 128
+PACK = 4
+K_PASS = P * PACK
+BATCHES, TOKENS, FEATURES = 2, 512, 1024
+PASSES = FEATURES // K_PASS
+BLOCKS = TOKENS // P
+ALL_BLOCKS = BATCHES * BLOCKS
+INV_DIVISOR = 1.0 / math.sqrt(128.0)
+
+FLOPS = 2 * 2 * BATCHES * TOKENS * FEATURES * FEATURES + 2 * BATCHES * TOKENS * TOKENS * FEATURES
+
+
+def tile_attentionnet_pa_kernel(tc, x, wq_words, wq_scales, wk_words, wk_scales, out):
+    nc = tc.nc
+    with ExitStack() as ctx:
+        keep = ctx.enter_context(tc.tile_pool(name="keep", bufs=1))
+        bank_pool = ctx.enter_context(tc.psum_pool(name="bank_pool", bufs=5))
+        score_pool = ctx.enter_context(tc.psum_pool(name="score_pool", bufs=3))
+        ctx.enter_context(tc.manual_schedule())
+
+        x_rows = keep.tile([P, ALL_BLOCKS, FEATURES], BF16)
+        x_grouped = keep.tile([P, ALL_BLOCKS, PASSES, P * PACK], BF16, align_bytes=64)
+        x_words = keep.tile([P, ALL_BLOCKS, PASSES, P], U32, align_bytes=64)
+        x_scales = keep.tile([P, ALL_BLOCKS, PASSES, P], U8, align_bytes=64)
+        wk_sb = keep.tile([P, PASSES, FEATURES], U32, align_bytes=64)
+        wq_sb = keep.tile([P, PASSES, FEATURES], U32, align_bytes=64)
+        wk_planes = keep.tile([P, PASSES, FEATURES], U8, align_bytes=64)
+        wq_planes = keep.tile([P, PASSES, FEATURES], U8, align_bytes=64)
+        k_grouped = keep.tile([P, BATCHES, PASSES, TOKENS, PACK], BF16, align_bytes=64)
+        k_words = keep.tile([P, BATCHES, PASSES, TOKENS], U32, align_bytes=64)
+        k_scales = keep.tile([P, BATCHES, PASSES, TOKENS], U8, align_bytes=64)
+        q_grouped = keep.tile([P, ALL_BLOCKS, PASSES, P, PACK], BF16, align_bytes=64)
+        q_words = keep.tile([P, ALL_BLOCKS, PASSES, P], U32, align_bytes=64)
+        q_scales = keep.tile([P, ALL_BLOCKS, PASSES, P], U8, align_bytes=64)
+        probs = keep.tile([P, ALL_BLOCKS, TOKENS], F32)
+        row_max = keep.tile([P, ALL_BLOCKS], F32)
+        exp_bias = keep.tile([P, ALL_BLOCKS], F32)
+        row_sum = keep.tile([P, ALL_BLOCKS], F32)
+        row_scale = keep.tile([P, ALL_BLOCKS], F32)
+        identity = keep.tile([P, P], F32)
+        table_warmer = keep.tile([P, 1], F32)
+
+        nc.vector.memset(wk_planes[:].bitcast(I32), 0)
+        nc.vector.memset(wq_planes[:].bitcast(I32), 0)
+        nc.vector.memset(table_warmer[:], 0.0)
+        nc.scalar.activation(out=table_warmer[:], in_=table_warmer[:], func=EXP)
+        make_identity(nc, identity[:])
+
+        x_view = x.rearrange("b (i p) d -> p (b i) d", p=P)
+
+        def load_x(b):
+            for half in range(2):
+                first = BLOCKS * b + 2 * half
+                nc.sync.dma_start(out=x_rows[:, first : first + 2, :], in_=x_view[:, first : first + 2, :])
+
+        def load_weight(words_sb, planes_sb, words, scales):
+            scale_rows = scales.rearrange("g (a r) n -> r a g n", r=4).bitcast(I32)
+            for r in range(4):
+                nc.sync.dma_start(out=planes_sb[r:P:32, :, :].bitcast(I32), in_=scale_rows[r])
+            word_rows = words.rearrange("g p n t -> p g (n t)").bitcast(I32)
+            for h in range(PASSES):
+                cols = slice(K_PASS * h, K_PASS * (h + 1))
+                nc.sync.dma_start(out=words_sb[:, :, cols].bitcast(I32), in_=word_rows[:, :, cols])
+
+        load_x(0)
+        load_weight(wk_sb, wk_planes, wk_words, wk_scales)
+        load_x(1)
+        load_weight(wq_sb, wq_planes, wq_words, wq_scales)
+
+        def leave_psum(on_vector, out_ap, in_ap):
+            if on_vector:
+                nc.vector.tensor_copy(out=out_ap, in_=in_ap)
+            else:
+                nc.scalar.copy(out=out_ap, in_=in_ap)
+
+        def quantise_x(i):
+            nc.vector.quantize_mx(
+                out=x_words[:, i, :, :].rearrange("p g c -> p (g c)").bitcast(FP8X4),
+                scales=x_scales[:, i, :, :].rearrange("p g c -> p (g c)"),
+                in_=x_grouped[:, i, :, :].rearrange("p g e -> p (g e)"),
+            )
+
+        def x_to_words(b):
+            for i in range(BLOCKS * b, BLOCKS * (b + 1)):
+                pairs = x_rows[:, i, :].bitcast(F32)
+                flipped = bank_pool.tile([P, PASSES, 2, P], F32, tag="bank")
+                for g in range(PASSES):
+                    for u in range(2):
+                        nc.tensor.transpose(
+                            flipped[:, g, u, :],
+                            pairs[:, (K_PASS // 2) * g + u : (K_PASS // 2) * (g + 1) : 2],
+                            identity[:],
+                        )
+                leave_psum(
+                    i % 2 == 1,
+                    x_grouped[:, i, :, :].bitcast(F32).rearrange("p g (c u) -> p g c u", u=2),
+                    flipped[:].rearrange("p g u c -> p g c u"),
+                )
+                if i > BLOCKS * b:
+                    quantise_x(i - 1)
+            quantise_x(BLOCKS * (b + 1) - 1)
+
+        def project(words_sb, planes_sb, i, h, on_vector, grouped_ap):
+            bank = bank_pool.tile([P, PACK, P], F32, tag="bank")
+            for t in range(PACK):
+                cols = slice(K_PASS * h + P * t, K_PASS * h + P * (t + 1))
+                for g in range(PASSES):
+                    nc.tensor.matmul_mx(
+                        out=bank[:, t, :],
+                        lhsT=words_sb[:, g, cols].bitcast(FP8X4),
+                        lhsT_scale=planes_sb[:, g, cols],
+                        rhs=x_words[:, i, g, :].bitcast(FP8X4),
+                        rhs_scale=x_scales[:, i, g, :],
+                        start=(g == 0),
+                        stop=(g == PASSES - 1),
+                    )
+            leave_psum(on_vector, grouped_ap, bank[:].rearrange("p t c -> p c t"))
+
+        def project_keys(b):
+            for h in range(PASSES):
+                for j in range(BLOCKS):
+                    project(wk_sb, wk_planes, BLOCKS * b + j, h, j % 2 == 1,
+                            k_grouped[:, b, h, P * j : P * (j + 1), :])
+                nc.vector.quantize_mx(
+                    out=k_words[:, b, h, :].bitcast(FP8X4),
+                    scales=k_scales[:, b, h, :],
+                    in_=k_grouped[:, b, h, :, :].rearrange("p c t -> p (c t)"),
+                )
+
+        def project_queries(i):
+            for h in range(PASSES):
+                project(wq_sb, wq_planes, i, h, False, q_grouped[:, i, h, :, :])
+            nc.vector.quantize_mx(
+                out=q_words[:, i, :, :].rearrange("p h c -> p (h c)").bitcast(FP8X4),
+                scales=q_scales[:, i, :, :].rearrange("p h c -> p (h c)"),
+                in_=q_grouped[:, i, :, :, :].rearrange("p h c t -> p (h c t)"),
+            )
+
+        scores = {}
+
+        def scores_and_maxima(i):
+            b = i // BLOCKS
+            scores[i] = score_pool.tile([P, TOKENS], F32, name="score_bank")
+            for h in range(PASSES):
+                nc.tensor.matmul_mx(
+                    out=scores[i][:],
+                    lhsT=q_words[:, i, h, :].bitcast(FP8X4),
+                    lhsT_scale=q_scales[:, i, h, :],
+                    rhs=k_words[:, b, h, :].bitcast(FP8X4),
+                    rhs_scale=k_scales[:, b, h, :],
+                    start=(h == 0),
+                    stop=(h == PASSES - 1),
+                )
+            nc.vector.tensor_reduce(out=row_max[:, i : i + 1], in_=scores[i][:], axis=ROW, op=MAX)
+            nc.vector.tensor_scalar(out=exp_bias[:, i : i + 1], in0=row_max[:, i : i + 1],
+                                    scalar1=-INV_DIVISOR, scalar2=None, op0=MULT)
+
+        def exponentials(i):
+            nc.scalar.activation(out=probs[:, i, :], in_=scores[i][:], func=EXP,
+                                 bias=exp_bias[:, i : i + 1], scale=INV_DIVISOR,
+                                 accum_out=row_sum[:, i : i + 1])
+
+        def normalise_and_store(i):
+            b, j = divmod(i, BLOCKS)
+            nc.vector.reciprocal(out=row_scale[:, i : i + 1], in_=row_sum[:, i : i + 1])
+            nc.vector.tensor_scalar_mul(out=probs[:, i, :], in0=probs[:, i, :], scalar1=row_scale[:, i : i + 1])
+            nc.sync.dma_start(out=out[b, P * j : P * (j + 1), :], in_=probs[:, i, :])
+
+        x_to_words(0)
+        for step in range(ALL_BLOCKS + 2):
+            if step >= 2:
+                exponentials(step - 2)
+            if step < ALL_BLOCKS:
+                b, j = divmod(step, BLOCKS)
+                if j == 0:
+                    project_keys(b)
+                    if b + 1 < BATCHES:
+                        x_to_words(b + 1)
+                project_queries(step)
+            if 1 <= step <= ALL_BLOCKS:
+                scores_and_maxima(step - 1)
+            if step >= 2:
+                normalise_and_store(step - 2)

@@ -66,9 +66,8 @@ def tile_attentionnet_pa_kernel(tc, x, wq_words, wq_scales, wk_words, wk_scales,
         x_view = x.rearrange("b (i p) d -> p (b i) d", p=P)
 
         def load_x(b):
-            for half in range(2):
-                first = BLOCKS * b + 2 * half
-                nc.sync.dma_start(out=x_rows[:, first : first + 2, :], in_=x_view[:, first : first + 2, :])
+            for i in range(BLOCKS * b, BLOCKS * (b + 1)):
+                nc.sync.dma_start(out=x_rows[:, i, :], in_=x_view[:, i, :])
 
         def load_weight(words_sb, planes_sb, words, scales):
             scale_rows = scales.rearrange("g (a r) n -> r a g n", r=4).bitcast(I32)
@@ -147,6 +146,8 @@ def tile_attentionnet_pa_kernel(tc, x, wq_words, wq_scales, wk_words, wk_scales,
         def project_queries(i):
             for h in range(PASSES):
                 project(wq_sb, wq_planes, i, h, False, q_grouped[:, i, h, :, :])
+
+        def quantise_queries(i):
             nc.vector.quantize_mx(
                 out=q_words[:, i, :, :].rearrange("p h c -> p (h c)").bitcast(FP8X4),
                 scales=q_scales[:, i, :, :].rearrange("p h c -> p (h c)"),
@@ -155,7 +156,7 @@ def tile_attentionnet_pa_kernel(tc, x, wq_words, wq_scales, wk_words, wk_scales,
 
         scores = {}
 
-        def scores_and_maxima(i):
+        def multiply_scores(i):
             b = i // BLOCKS
             scores[i] = score_pool.tile([P, TOKENS], F32, name="score_bank")
             for h in range(PASSES):
@@ -168,6 +169,8 @@ def tile_attentionnet_pa_kernel(tc, x, wq_words, wq_scales, wk_words, wk_scales,
                     start=(h == 0),
                     stop=(h == PASSES - 1),
                 )
+
+        def maxima(i):
             nc.vector.tensor_reduce(out=row_max[:, i : i + 1], in_=scores[i][:], axis=ROW, op=MAX)
             nc.vector.tensor_scalar(out=exp_bias[:, i : i + 1], in0=row_max[:, i : i + 1],
                                     scalar1=-INV_DIVISOR, scalar2=None, op0=MULT)
@@ -184,9 +187,9 @@ def tile_attentionnet_pa_kernel(tc, x, wq_words, wq_scales, wk_words, wk_scales,
             nc.sync.dma_start(out=out[b, P * j : P * (j + 1), :], in_=probs[:, i, :])
 
         x_to_words(0)
-        for step in range(ALL_BLOCKS + 2):
-            if step >= 2:
-                exponentials(step - 2)
+        for step in range(ALL_BLOCKS + 3):
+            if step >= 3:
+                exponentials(step - 3)
             if step < ALL_BLOCKS:
                 b, j = divmod(step, BLOCKS)
                 if j == 0:
@@ -195,6 +198,9 @@ def tile_attentionnet_pa_kernel(tc, x, wq_words, wq_scales, wk_words, wk_scales,
                         x_to_words(b + 1)
                 project_queries(step)
             if 1 <= step <= ALL_BLOCKS:
-                scores_and_maxima(step - 1)
-            if step >= 2:
-                normalise_and_store(step - 2)
+                quantise_queries(step - 1)
+                multiply_scores(step - 1)
+            if 2 <= step <= ALL_BLOCKS + 1:
+                maxima(step - 2)
+            if step >= 3:
+                normalise_and_store(step - 3)

@@ -132,11 +132,12 @@ def tile_attentionnet_pa_kernel(tc, x, wq_words, wq_scales, wk_words, wk_scales,
                     )
             leave_psum(on_vector, grouped_ap, bank[:].rearrange("p t c -> p c t"))
 
-        def project_keys(b):
-            for h in range(PASSES):
-                for j in range(BLOCKS):
-                    project(wk_sb, wk_planes, BLOCKS * b + j, h, j % 2 == 1,
-                            k_grouped[:, b, h, P * j : P * (j + 1), :])
+        def project_keys(b, quarter):
+            h, half = divmod(quarter, 2)
+            for j in (2 * half, 2 * half + 1):
+                project(wk_sb, wk_planes, BLOCKS * b + j, h, j % 2 == 1,
+                        k_grouped[:, b, h, P * j : P * (j + 1), :])
+            if half == 1:
                 nc.vector.quantize_mx(
                     out=k_words[:, b, h, :].bitcast(FP8X4),
                     scales=k_scales[:, b, h, :],
@@ -148,11 +149,12 @@ def tile_attentionnet_pa_kernel(tc, x, wq_words, wq_scales, wk_words, wk_scales,
                 project(wq_sb, wq_planes, i, h, False, q_grouped[:, i, h, :, :])
 
         def quantise_queries(i):
-            nc.vector.quantize_mx(
-                out=q_words[:, i, :, :].rearrange("p h c -> p (h c)").bitcast(FP8X4),
-                scales=q_scales[:, i, :, :].rearrange("p h c -> p (h c)"),
-                in_=q_grouped[:, i, :, :, :].rearrange("p h c t -> p (h c t)"),
-            )
+            for h in range(PASSES):
+                nc.vector.quantize_mx(
+                    out=q_words[:, i, h, :].bitcast(FP8X4),
+                    scales=q_scales[:, i, h, :],
+                    in_=q_grouped[:, i, h, :, :].rearrange("p c t -> p (c t)"),
+                )
 
         scores = {}
 
@@ -172,6 +174,8 @@ def tile_attentionnet_pa_kernel(tc, x, wq_words, wq_scales, wk_words, wk_scales,
 
         def maxima(i):
             nc.vector.tensor_reduce(out=row_max[:, i : i + 1], in_=scores[i][:], axis=ROW, op=MAX)
+
+        def exp_biases(i):
             nc.vector.tensor_scalar(out=exp_bias[:, i : i + 1], in0=row_max[:, i : i + 1],
                                     scalar1=-INV_DIVISOR, scalar2=None, op0=MULT)
 
@@ -180,27 +184,34 @@ def tile_attentionnet_pa_kernel(tc, x, wq_words, wq_scales, wk_words, wk_scales,
                                  bias=exp_bias[:, i : i + 1], scale=INV_DIVISOR,
                                  accum_out=row_sum[:, i : i + 1])
 
-        def normalise_and_store(i):
-            b, j = divmod(i, BLOCKS)
+        def reciprocals(i):
             nc.vector.reciprocal(out=row_scale[:, i : i + 1], in_=row_sum[:, i : i + 1])
+
+        def scale_and_store(i):
+            b, j = divmod(i, BLOCKS)
             nc.vector.tensor_scalar_mul(out=probs[:, i, :], in0=probs[:, i, :], scalar1=row_scale[:, i : i + 1])
             nc.sync.dma_start(out=out[b, P * j : P * (j + 1), :], in_=probs[:, i, :])
 
         x_to_words(0)
+        for quarter in range(BLOCKS):
+            project_keys(0, quarter)
+        x_to_words(1)
         for step in range(ALL_BLOCKS + 3):
             if step >= 3:
                 exponentials(step - 3)
             if step < ALL_BLOCKS:
-                b, j = divmod(step, BLOCKS)
-                if j == 0:
-                    project_keys(b)
-                    if b + 1 < BATCHES:
-                        x_to_words(b + 1)
                 project_queries(step)
             if 1 <= step <= ALL_BLOCKS:
                 quantise_queries(step - 1)
-                multiply_scores(step - 1)
             if 2 <= step <= ALL_BLOCKS + 1:
                 maxima(step - 2)
             if step >= 3:
-                normalise_and_store(step - 3)
+                reciprocals(step - 3)
+            if 2 <= step <= ALL_BLOCKS + 1:
+                exp_biases(step - 2)
+            if step >= 3:
+                scale_and_store(step - 3)
+            if step < BLOCKS:
+                project_keys(1, step)
+            if 1 <= step <= ALL_BLOCKS:
+                multiply_scores(step - 1)

@@ -23,6 +23,7 @@ PASSES = FEATURES // K_PASS
 BLOCKS = TOKENS // P
 ALL_BLOCKS = BATCHES * BLOCKS
 INV_DIVISOR = 1.0 / math.sqrt(128.0)
+WARM_UP = 4
 
 FLOPS = 2 * 2 * BATCHES * TOKENS * FEATURES * FEATURES + 2 * BATCHES * TOKENS * TOKENS * FEATURES
 
@@ -56,7 +57,9 @@ def tile_attentionnet_pa_kernel(tc, x, wq_words, wq_scales, wk_words, wk_scales,
         row_scale = keep.tile([P, ALL_BLOCKS], F32)
         identity = keep.tile([P, P], F32)
         table_warmer = keep.tile([P, 1], F32)
+        zeros = keep.tile([P, TOKENS], BF16)
 
+        nc.vector.memset(zeros[:], 0.0)
         nc.vector.memset(wk_planes[:].bitcast(I32), 0)
         nc.vector.memset(wq_planes[:].bitcast(I32), 0)
         nc.vector.memset(table_warmer[:], 0.0)
@@ -69,19 +72,18 @@ def tile_attentionnet_pa_kernel(tc, x, wq_words, wq_scales, wk_words, wk_scales,
             for i in range(BLOCKS * b, BLOCKS * (b + 1)):
                 nc.sync.dma_start(out=x_rows[:, i, :], in_=x_view[:, i, :])
 
-        def load_weight(words_sb, planes_sb, words, scales):
+        def load_weight(words_sb, planes_sb, words, scales, column_cuts):
             scale_rows = scales.rearrange("g (a r) n -> r a g n", r=4).bitcast(I32)
             for r in range(4):
                 nc.sync.dma_start(out=planes_sb[r:P:32, :, :].bitcast(I32), in_=scale_rows[r])
             word_rows = words.rearrange("g p n t -> p g (n t)").bitcast(I32)
-            for h in range(PASSES):
-                cols = slice(K_PASS * h, K_PASS * (h + 1))
-                nc.sync.dma_start(out=words_sb[:, :, cols].bitcast(I32), in_=word_rows[:, :, cols])
+            for first, last in zip(column_cuts[:-1], column_cuts[1:]):
+                nc.sync.dma_start(out=words_sb[:, :, first:last].bitcast(I32), in_=word_rows[:, :, first:last])
 
         load_x(0)
-        load_weight(wk_sb, wk_planes, wk_words, wk_scales)
+        load_weight(wk_sb, wk_planes, wk_words, wk_scales, (0, K_PASS // 2, K_PASS, FEATURES))
         load_x(1)
-        load_weight(wq_sb, wq_planes, wq_words, wq_scales)
+        load_weight(wq_sb, wq_planes, wq_words, wq_scales, (0, K_PASS, FEATURES))
 
         def leave_psum(on_vector, out_ap, in_ap):
             if on_vector:
@@ -116,21 +118,35 @@ def tile_attentionnet_pa_kernel(tc, x, wq_words, wq_scales, wk_words, wk_scales,
                     quantise_x(i - 1)
             quantise_x(BLOCKS * (b + 1) - 1)
 
+        def multiply_weights(bank, words_sb, planes_sb, i, h, t):
+            cols = slice(K_PASS * h + P * t, K_PASS * h + P * (t + 1))
+            for g in range(PASSES):
+                nc.tensor.matmul_mx(
+                    out=bank[:, t, :],
+                    lhsT=words_sb[:, g, cols].bitcast(FP8X4),
+                    lhsT_scale=planes_sb[:, g, cols],
+                    rhs=x_words[:, i, g, :].bitcast(FP8X4),
+                    rhs_scale=x_scales[:, i, g, :],
+                    start=(g == 0),
+                    stop=(g == PASSES - 1),
+                )
+
         def project(words_sb, planes_sb, i, h, on_vector, grouped_ap):
             bank = bank_pool.tile([P, PACK, P], F32, tag="bank")
             for t in range(PACK):
-                cols = slice(K_PASS * h + P * t, K_PASS * h + P * (t + 1))
-                for g in range(PASSES):
-                    nc.tensor.matmul_mx(
-                        out=bank[:, t, :],
-                        lhsT=words_sb[:, g, cols].bitcast(FP8X4),
-                        lhsT_scale=planes_sb[:, g, cols],
-                        rhs=x_words[:, i, g, :].bitcast(FP8X4),
-                        rhs_scale=x_scales[:, i, g, :],
-                        start=(g == 0),
-                        stop=(g == PASSES - 1),
-                    )
+                multiply_weights(bank, words_sb, planes_sb, i, h, t)
             leave_psum(on_vector, grouped_ap, bank[:].rearrange("p t c -> p c t"))
+
+        def project_first_keys():
+            pair = (0, 1)
+            banks = {}
+            for j in pair:
+                banks[j] = bank_pool.tile([P, PACK, P], F32, tag="bank", name="first_bank")
+            for t in range(PACK):
+                for j in pair:
+                    multiply_weights(banks[j], wk_sb, wk_planes, j, 0, t)
+            for j in pair:
+                leave_psum(j % 2 == 1, k_grouped[:, 0, 0, P * j : P * (j + 1), :], banks[j][:].rearrange("p t c -> p c t"))
 
         def project_keys(b, quarter):
             h, half = divmod(quarter, 2)
@@ -192,8 +208,12 @@ def tile_attentionnet_pa_kernel(tc, x, wq_words, wq_scales, wk_words, wk_scales,
             nc.vector.tensor_scalar_mul(out=probs[:, i, :], in0=probs[:, i, :], scalar1=row_scale[:, i : i + 1])
             nc.sync.dma_start(out=out[b, P * j : P * (j + 1), :], in_=probs[:, i, :])
 
+        idle_bank = bank_pool.tile([P, TOKENS], F32, tag="bank")
+        for _ in range(WARM_UP):
+            nc.tensor.matmul(out=idle_bank[:], lhsT=zeros[:, :P], rhs=zeros[:], start=True, stop=True)
         x_to_words(0)
-        for quarter in range(BLOCKS):
+        project_first_keys()
+        for quarter in range(1, BLOCKS):
             project_keys(0, quarter)
         x_to_words(1)
         for step in range(ALL_BLOCKS + 3):

@@ -13,6 +13,7 @@ FP8X4 = mybir.dt.float8_e4m3fn_x4
 EXP = mybir.ActivationFunctionType.Exp
 MAX = mybir.AluOpType.max
 MULT = mybir.AluOpType.mult
+ADD = mybir.AluOpType.add
 ROW = mybir.AxisListType.X
 
 P = 128
@@ -37,6 +38,7 @@ def tile_attentionnet_pa_kernel(tc, x, wq_words, wq_scales, wk_words, wk_scales,
         ctx.enter_context(tc.manual_schedule())
 
         x_rows = keep.tile([P, ALL_BLOCKS, FEATURES], BF16)
+        x_sorted = keep.tile([P, BLOCKS, PASSES, 2, P], F32)
         x_grouped = keep.tile([P, ALL_BLOCKS, PASSES, P * PACK], BF16, align_bytes=64)
         x_words = keep.tile([P, ALL_BLOCKS, PASSES, P], U32, align_bytes=64)
         x_scales = keep.tile([P, ALL_BLOCKS, PASSES, P], U8, align_bytes=64)
@@ -98,17 +100,23 @@ def tile_attentionnet_pa_kernel(tc, x, wq_words, wq_scales, wk_words, wk_scales,
                 in_=x_grouped[:, i, :, :].rearrange("p g e -> p (g e)"),
             )
 
+        def sort_words(i):
+            nc.scalar.copy(
+                out=x_sorted[:, i - BLOCKS, :, :, :],
+                in_=x_rows[:, i, :].bitcast(F32).rearrange("p (g c u) -> p g u c", g=PASSES, u=2),
+            )
+
         def x_to_words(b):
             for i in range(BLOCKS * b, BLOCKS * (b + 1)):
                 pairs = x_rows[:, i, :].bitcast(F32)
                 flipped = bank_pool.tile([P, PASSES, 2, P], F32, tag="bank")
                 for g in range(PASSES):
                     for u in range(2):
-                        nc.tensor.transpose(
-                            flipped[:, g, u, :],
-                            pairs[:, (K_PASS // 2) * g + u : (K_PASS // 2) * (g + 1) : 2],
-                            identity[:],
-                        )
+                        if b == 0:
+                            words = pairs[:, (K_PASS // 2) * g + u : (K_PASS // 2) * (g + 1) : 2]
+                        else:
+                            words = x_sorted[:, i - BLOCKS, g, u, :]
+                        nc.tensor.transpose(flipped[:, g, u, :], words, identity[:])
                 leave_psum(
                     i % 2 == 1,
                     x_grouped[:, i, :, :].bitcast(F32).rearrange("p g (c u) -> p g c u", u=2),
@@ -205,16 +213,31 @@ def tile_attentionnet_pa_kernel(tc, x, wq_words, wq_scales, wk_words, wk_scales,
 
         def scale_and_store(i):
             b, j = divmod(i, BLOCKS)
-            nc.vector.tensor_scalar_mul(out=probs[:, i, :], in0=probs[:, i, :], scalar1=row_scale[:, i : i + 1])
-            nc.sync.dma_start(out=out[b, P * j : P * (j + 1), :], in_=probs[:, i, :])
+            rows = out[b, P * j : P * (j + 1), :]
+            if i == ALL_BLOCKS - 1:
+                for cols in (slice(0, TOKENS // 2), slice(TOKENS // 2, TOKENS)):
+                    nc.vector.tensor_scalar_mul(out=probs[:, i, cols], in0=probs[:, i, cols], scalar1=row_scale[:, i : i + 1])
+                    nc.sync.dma_start(out=rows[:, cols], in_=probs[:, i, cols])
+                return
+            if i == ALL_BLOCKS - 3:
+                nc.gpsimd.tensor_scalar(out=probs[:, i, :], in0=probs[:, i, :], scalar1=row_scale[:, i : i + 1],
+                                        scalar2=0.0, op0=MULT, op1=ADD)
+            else:
+                nc.vector.tensor_scalar_mul(out=probs[:, i, :], in0=probs[:, i, :], scalar1=row_scale[:, i : i + 1])
+            nc.sync.dma_start(out=rows, in_=probs[:, i, :])
 
         idle_bank = bank_pool.tile([P, TOKENS], F32, tag="bank")
         for _ in range(WARM_UP):
             nc.tensor.matmul(out=idle_bank[:], lhsT=zeros[:, :P], rhs=zeros[:], start=True, stop=True)
         x_to_words(0)
         project_first_keys()
-        for quarter in range(1, BLOCKS):
-            project_keys(0, quarter)
+        project_keys(0, 1)
+        sort_words(BLOCKS)
+        project_keys(0, 2)
+        sort_words(BLOCKS + 1)
+        project_keys(0, 3)
+        sort_words(BLOCKS + 2)
+        sort_words(BLOCKS + 3)
         x_to_words(1)
         for step in range(ALL_BLOCKS + 3):
             if step >= 3:
@@ -225,9 +248,11 @@ def tile_attentionnet_pa_kernel(tc, x, wq_words, wq_scales, wk_words, wk_scales,
                 quantise_queries(step - 1)
             if 2 <= step <= ALL_BLOCKS + 1:
                 maxima(step - 2)
+            if step == ALL_BLOCKS + 1:
+                exp_biases(step - 2)
             if step >= 3:
                 reciprocals(step - 3)
-            if 2 <= step <= ALL_BLOCKS + 1:
+            if 2 <= step <= ALL_BLOCKS:
                 exp_biases(step - 2)
             if step >= 3:
                 scale_and_store(step - 3)

@@ -100,10 +100,11 @@ def tile_attentionnet_pa_kernel(tc, x, wq_words, wq_scales, wk_words, wk_scales,
                 in_=x_grouped[:, i, :, :].rearrange("p g e -> p (g e)"),
             )
 
-        def sort_words(i):
-            nc.scalar.copy(
-                out=x_sorted[:, i - BLOCKS, :, :, :],
-                in_=x_rows[:, i, :].bitcast(F32).rearrange("p (g c u) -> p g u c", g=PASSES, u=2),
+        def sort_words(i, on_vector):
+            leave_psum(
+                on_vector,
+                x_sorted[:, i - BLOCKS, :, :, :],
+                x_rows[:, i, :].bitcast(F32).rearrange("p (g c u) -> p g u c", g=PASSES, u=2),
             )
 
         def x_to_words(b):
@@ -156,17 +157,15 @@ def tile_attentionnet_pa_kernel(tc, x, wq_words, wq_scales, wk_words, wk_scales,
             for j in pair:
                 leave_psum(j % 2 == 1, k_grouped[:, 0, 0, P * j : P * (j + 1), :], banks[j][:].rearrange("p t c -> p c t"))
 
-        def project_keys(b, quarter):
-            h, half = divmod(quarter, 2)
-            for j in (2 * half, 2 * half + 1):
-                project(wk_sb, wk_planes, BLOCKS * b + j, h, j % 2 == 1,
-                        k_grouped[:, b, h, P * j : P * (j + 1), :])
-            if half == 1:
-                nc.vector.quantize_mx(
-                    out=k_words[:, b, h, :].bitcast(FP8X4),
-                    scales=k_scales[:, b, h, :],
-                    in_=k_grouped[:, b, h, :, :].rearrange("p c t -> p (c t)"),
-                )
+        def project_keys(b, h, j, on_vector):
+            project(wk_sb, wk_planes, BLOCKS * b + j, h, on_vector, k_grouped[:, b, h, P * j : P * (j + 1), :])
+
+        def quantise_keys(b, h):
+            nc.vector.quantize_mx(
+                out=k_words[:, b, h, :].bitcast(FP8X4),
+                scales=k_scales[:, b, h, :],
+                in_=k_grouped[:, b, h, :, :].rearrange("p c t -> p (c t)"),
+            )
 
         def project_queries(i):
             for h in range(PASSES):
@@ -231,14 +230,22 @@ def tile_attentionnet_pa_kernel(tc, x, wq_words, wq_scales, wk_words, wk_scales,
             nc.tensor.matmul(out=idle_bank[:], lhsT=zeros[:, :P], rhs=zeros[:], start=True, stop=True)
         x_to_words(0)
         project_first_keys()
-        project_keys(0, 1)
-        sort_words(BLOCKS)
-        project_keys(0, 2)
-        sort_words(BLOCKS + 1)
-        project_keys(0, 3)
-        sort_words(BLOCKS + 2)
-        sort_words(BLOCKS + 3)
+        project_keys(0, 0, 2, False)
+        project_keys(0, 0, 3, True)
+        quantise_keys(0, 0)
+        sort_words(BLOCKS, False)
+        project_keys(0, 1, 0, False)
+        project_keys(0, 1, 1, True)
+        sort_words(BLOCKS + 1, False)
+        project_keys(0, 1, 2, False)
+        sort_words(BLOCKS + 2, True)
+        sort_words(BLOCKS + 3, True)
         x_to_words(1)
+        project_keys(0, 1, 3, False)
+        quantise_keys(0, 1)
+        for j in range(BLOCKS):
+            project_keys(1, 0, j, j == BLOCKS - 1)
+        quantise_keys(1, 0)
         for step in range(ALL_BLOCKS + 3):
             if step >= 3:
                 exponentials(step - 3)
@@ -257,6 +264,8 @@ def tile_attentionnet_pa_kernel(tc, x, wq_words, wq_scales, wk_words, wk_scales,
             if step >= 3:
                 scale_and_store(step - 3)
             if step < BLOCKS:
-                project_keys(1, step)
+                project_keys(1, 1, step, True)
+            if step == BLOCKS - 1:
+                quantise_keys(1, 1)
             if 1 <= step <= ALL_BLOCKS:
                 multiply_scores(step - 1)

@@ -38,7 +38,6 @@ def tile_attentionnet_pa_kernel(tc, x, wq_words, wq_scales, wk_words, wk_scales,
         ctx.enter_context(tc.manual_schedule())
 
         x_rows = keep.tile([P, ALL_BLOCKS, FEATURES], BF16)
-        x_sorted = keep.tile([P, BLOCKS, PASSES, 2, P], F32)
         x_grouped = keep.tile([P, ALL_BLOCKS, PASSES, P * PACK], BF16, align_bytes=64)
         x_words = keep.tile([P, ALL_BLOCKS, PASSES, P], U32, align_bytes=64)
         x_scales = keep.tile([P, ALL_BLOCKS, PASSES, P], U8, align_bytes=64)
@@ -100,24 +99,17 @@ def tile_attentionnet_pa_kernel(tc, x, wq_words, wq_scales, wk_words, wk_scales,
                 in_=x_grouped[:, i, :, :].rearrange("p g e -> p (g e)"),
             )
 
-        def sort_words(i, on_vector):
-            leave_psum(
-                on_vector,
-                x_sorted[:, i - BLOCKS, :, :, :],
-                x_rows[:, i, :].bitcast(F32).rearrange("p (g c u) -> p g u c", g=PASSES, u=2),
-            )
-
         def x_to_words(b):
             for i in range(BLOCKS * b, BLOCKS * (b + 1)):
                 pairs = x_rows[:, i, :].bitcast(F32)
                 flipped = bank_pool.tile([P, PASSES, 2, P], F32, tag="bank")
                 for g in range(PASSES):
                     for u in range(2):
-                        if b == 0:
-                            words = pairs[:, (K_PASS // 2) * g + u : (K_PASS // 2) * (g + 1) : 2]
-                        else:
-                            words = x_sorted[:, i - BLOCKS, g, u, :]
-                        nc.tensor.transpose(flipped[:, g, u, :], words, identity[:])
+                        nc.tensor.transpose(
+                            flipped[:, g, u, :],
+                            pairs[:, (K_PASS // 2) * g + u : (K_PASS // 2) * (g + 1) : 2],
+                            identity[:],
+                        )
                 leave_psum(
                     i % 2 == 1,
                     x_grouped[:, i, :, :].bitcast(F32).rearrange("p g (c u) -> p g c u", u=2),
@@ -233,13 +225,9 @@ def tile_attentionnet_pa_kernel(tc, x, wq_words, wq_scales, wk_words, wk_scales,
         project_keys(0, 0, 2, False)
         project_keys(0, 0, 3, True)
         quantise_keys(0, 0)
-        sort_words(BLOCKS, False)
         project_keys(0, 1, 0, False)
         project_keys(0, 1, 1, True)
-        sort_words(BLOCKS + 1, False)
         project_keys(0, 1, 2, False)
-        sort_words(BLOCKS + 2, True)
-        sort_words(BLOCKS + 3, True)
         x_to_words(1)
         project_keys(0, 1, 3, False)
         quantise_keys(0, 1)

@@ -251,9 +251,9 @@ def tile_attentionnet_pa_kernel(tc, x, wq_words, wq_scales, wk_words, wk_scales,
                 exp_biases(step - 2)
             if step >= 3:
                 scale_and_store(step - 3)
-            if step < BLOCKS:
-                project_keys(1, 1, step, True)
-            if step == BLOCKS - 1:
+            if 1 <= step <= BLOCKS:
+                project_keys(1, 1, step - 1, True)
+            if step == BLOCKS:
                 quantise_keys(1, 1)
             if 1 <= step <= ALL_BLOCKS:
                 multiply_scores(step - 1)

@@ -11,10 +11,9 @@ U32 = mybir.dt.uint32
 U8 = mybir.dt.uint8
 FP8X4 = mybir.dt.float8_e4m3fn_x4
 EXP = mybir.ActivationFunctionType.Exp
-MAX = mybir.AluOpType.max
+MIN = mybir.AluOpType.min
 MULT = mybir.AluOpType.mult
 ADD = mybir.AluOpType.add
-ROW = mybir.AxisListType.X
 
 P = 128
 PACK = 4
@@ -52,7 +51,7 @@ def tile_attentionnet_pa_kernel(tc, x, wq_words, wq_scales, wk_words, wk_scales,
         q_words = keep.tile([P, ALL_BLOCKS, PASSES, P], U32, align_bytes=64)
         q_scales = keep.tile([P, ALL_BLOCKS, PASSES, P], U8, align_bytes=64)
         probs = keep.tile([P, ALL_BLOCKS, TOKENS], F32)
-        row_max = keep.tile([P, ALL_BLOCKS], F32)
+        unused = keep.tile([P, TOKENS], BF16)
         exp_bias = keep.tile([P, ALL_BLOCKS], F32)
         row_sum = keep.tile([P, ALL_BLOCKS], F32)
         row_scale = keep.tile([P, ALL_BLOCKS], F32)
@@ -188,11 +187,8 @@ def tile_attentionnet_pa_kernel(tc, x, wq_words, wq_scales, wk_words, wk_scales,
                 )
 
         def maxima(i):
-            nc.vector.tensor_reduce(out=row_max[:, i : i + 1], in_=scores[i][:], axis=ROW, op=MAX)
-
-        def exp_biases(i):
-            nc.vector.tensor_scalar(out=exp_bias[:, i : i + 1], in0=row_max[:, i : i + 1],
-                                    scalar1=-INV_DIVISOR, scalar2=None, op0=MULT)
+            nc.vector.tensor_scalar(out=unused[:], in0=scores[i][:], scalar1=-INV_DIVISOR, scalar2=None,
+                                    op0=MULT, op1=MIN, accum_out=exp_bias[:, i : i + 1])
 
         def exponentials(i):
             nc.scalar.activation(out=probs[:, i, :], in_=scores[i][:], func=EXP,
@@ -243,12 +239,8 @@ def tile_attentionnet_pa_kernel(tc, x, wq_words, wq_scales, wk_words, wk_scales,
                 quantise_queries(step - 1)
             if 2 <= step <= ALL_BLOCKS + 1:
                 maxima(step - 2)
-            if step == ALL_BLOCKS + 1:
-                exp_biases(step - 2)
             if step >= 3:
                 reciprocals(step - 3)
-            if 2 <= step <= ALL_BLOCKS:
-                exp_biases(step - 2)
             if step >= 3:
                 scale_and_store(step - 3)
             if 1 <= step <= BLOCKS:

@@ -32,8 +32,8 @@ def tile_attentionnet_pa_kernel(tc, x, wq_words, wq_scales, wk_words, wk_scales,
     nc = tc.nc
     with ExitStack() as ctx:
         keep = ctx.enter_context(tc.tile_pool(name="keep", bufs=1))
-        bank_pool = ctx.enter_context(tc.psum_pool(name="bank_pool", bufs=5))
-        score_pool = ctx.enter_context(tc.psum_pool(name="score_pool", bufs=3))
+        bank_pool = ctx.enter_context(tc.psum_pool(name="bank_pool", bufs=6))
+        score_pool = ctx.enter_context(tc.psum_pool(name="score_pool", bufs=2))
         ctx.enter_context(tc.manual_schedule())
 
         x_rows = keep.tile([P, ALL_BLOCKS, FEATURES], BF16)
@@ -51,7 +51,7 @@ def tile_attentionnet_pa_kernel(tc, x, wq_words, wq_scales, wk_words, wk_scales,
         q_words = keep.tile([P, ALL_BLOCKS, PASSES, P], U32, align_bytes=64)
         q_scales = keep.tile([P, ALL_BLOCKS, PASSES, P], U8, align_bytes=64)
         probs = keep.tile([P, ALL_BLOCKS, TOKENS], F32)
-        unused = keep.tile([P, TOKENS], BF16)
+        scaled = keep.tile([P, ALL_BLOCKS, TOKENS], F32)
         exp_bias = keep.tile([P, ALL_BLOCKS], F32)
         row_sum = keep.tile([P, ALL_BLOCKS], F32)
         row_scale = keep.tile([P, ALL_BLOCKS], F32)
@@ -187,12 +187,12 @@ def tile_attentionnet_pa_kernel(tc, x, wq_words, wq_scales, wk_words, wk_scales,
                 )
 
         def maxima(i):
-            nc.vector.tensor_scalar(out=unused[:], in0=scores[i][:], scalar1=-INV_DIVISOR, scalar2=None,
+            nc.vector.tensor_scalar(out=scaled[:, i, :], in0=scores[i][:], scalar1=-INV_DIVISOR, scalar2=None,
                                     op0=MULT, op1=MIN, accum_out=exp_bias[:, i : i + 1])
 
         def exponentials(i):
-            nc.scalar.activation(out=probs[:, i, :], in_=scores[i][:], func=EXP,
-                                 bias=exp_bias[:, i : i + 1], scale=INV_DIVISOR,
+            nc.scalar.activation(out=probs[:, i, :], in_=scaled[:, i, :], func=EXP,
+                                 bias=exp_bias[:, i : i + 1], scale=-1.0,
                                  accum_out=row_sum[:, i : i + 1])
 
         def reciprocals(i):

from contextlib import ExitStack
import math

import concourse.mybir as mybir
from concourse.masks import make_identity

F32 = mybir.dt.float32
BF16 = mybir.dt.bfloat16
I32 = mybir.dt.int32
U32 = mybir.dt.uint32
U8 = mybir.dt.uint8
FP8X4 = mybir.dt.float8_e4m3fn_x4
EXP = mybir.ActivationFunctionType.Exp
MIN = mybir.AluOpType.min
MULT = mybir.AluOpType.mult
ADD = mybir.AluOpType.add

P = 128
PACK = 4
K_PASS = P * PACK
BATCHES, TOKENS, FEATURES = 2, 512, 1024
PASSES = FEATURES // K_PASS
BLOCKS = TOKENS // P
ALL_BLOCKS = BATCHES * BLOCKS
INV_DIVISOR = 1.0 / math.sqrt(128.0)
WARM_UP = 4

FLOPS = 2 * 2 * BATCHES * TOKENS * FEATURES * FEATURES + 2 * BATCHES * TOKENS * TOKENS * FEATURES


def tile_attentionnet_pa_kernel(tc, x, wq_words, wq_scales, wk_words, wk_scales, out):
    nc = tc.nc
    with ExitStack() as ctx:
        keep = ctx.enter_context(tc.tile_pool(name="keep", bufs=1))
        bank_pool = ctx.enter_context(tc.psum_pool(name="bank_pool", bufs=6))
        score_pool = ctx.enter_context(tc.psum_pool(name="score_pool", bufs=2))
        ctx.enter_context(tc.manual_schedule())

        x_rows = keep.tile([P, ALL_BLOCKS, FEATURES], BF16)
        x_grouped = keep.tile([P, ALL_BLOCKS, PASSES, P * PACK], BF16, align_bytes=64)
        x_words = keep.tile([P, ALL_BLOCKS, PASSES, P], U32, align_bytes=64)
        x_scales = keep.tile([P, ALL_BLOCKS, PASSES, P], U8, align_bytes=64)
        wk_sb = keep.tile([P, PASSES, FEATURES], U32, align_bytes=64)
        wq_sb = keep.tile([P, PASSES, FEATURES], U32, align_bytes=64)
        wk_planes = keep.tile([P, PASSES, FEATURES], U8, align_bytes=64)
        wq_planes = keep.tile([P, PASSES, FEATURES], U8, align_bytes=64)
        k_grouped = keep.tile([P, BATCHES, PASSES, TOKENS, PACK], BF16, align_bytes=64)
        k_words = keep.tile([P, BATCHES, PASSES, TOKENS], U32, align_bytes=64)
        k_scales = keep.tile([P, BATCHES, PASSES, TOKENS], U8, align_bytes=64)
        q_grouped = keep.tile([P, ALL_BLOCKS, PASSES, P, PACK], BF16, align_bytes=64)
        q_words = keep.tile([P, ALL_BLOCKS, PASSES, P], U32, align_bytes=64)
        q_scales = keep.tile([P, ALL_BLOCKS, PASSES, P], U8, align_bytes=64)
        probs = keep.tile([P, ALL_BLOCKS, TOKENS], F32)
        scaled = keep.tile([P, ALL_BLOCKS, TOKENS], F32)
        exp_bias = keep.tile([P, ALL_BLOCKS], F32)
        row_sum = keep.tile([P, ALL_BLOCKS], F32)
        row_scale = keep.tile([P, ALL_BLOCKS], F32)
        identity = keep.tile([P, P], F32)
        table_warmer = keep.tile([P, 1], F32)
        zeros = keep.tile([P, TOKENS], BF16)

        nc.vector.memset(zeros[:], 0.0)
        nc.vector.memset(wk_planes[:].bitcast(I32), 0)
        nc.vector.memset(wq_planes[:].bitcast(I32), 0)
        nc.vector.memset(table_warmer[:], 0.0)
        nc.scalar.activation(out=table_warmer[:], in_=table_warmer[:], func=EXP)
        make_identity(nc, identity[:])

        x_view = x.rearrange("b (i p) d -> p (b i) d", p=P)

        def load_x(b):
            for i in range(BLOCKS * b, BLOCKS * (b + 1)):
                nc.sync.dma_start(out=x_rows[:, i, :], in_=x_view[:, i, :])

        def load_weight(words_sb, planes_sb, words, scales, column_cuts):
            scale_rows = scales.rearrange("g (a r) n -> r a g n", r=4).bitcast(I32)
            for r in range(4):
                nc.sync.dma_start(out=planes_sb[r:P:32, :, :].bitcast(I32), in_=scale_rows[r])
            word_rows = words.rearrange("g p n t -> p g (n t)").bitcast(I32)
            for first, last in zip(column_cuts[:-1], column_cuts[1:]):
                nc.sync.dma_start(out=words_sb[:, :, first:last].bitcast(I32), in_=word_rows[:, :, first:last])

        load_x(0)
        load_weight(wk_sb, wk_planes, wk_words, wk_scales, (0, K_PASS // 2, K_PASS, FEATURES))
        load_x(1)
        load_weight(wq_sb, wq_planes, wq_words, wq_scales, (0, K_PASS, FEATURES))

        def leave_psum(on_vector, out_ap, in_ap):
            if on_vector:
                nc.vector.tensor_copy(out=out_ap, in_=in_ap)
            else:
                nc.scalar.copy(out=out_ap, in_=in_ap)

        def quantise_x(i):
            nc.vector.quantize_mx(
                out=x_words[:, i, :, :].rearrange("p g c -> p (g c)").bitcast(FP8X4),
                scales=x_scales[:, i, :, :].rearrange("p g c -> p (g c)"),
                in_=x_grouped[:, i, :, :].rearrange("p g e -> p (g e)"),
            )

        def x_to_words(b):
            for i in range(BLOCKS * b, BLOCKS * (b + 1)):
                pairs = x_rows[:, i, :].bitcast(F32)
                flipped = bank_pool.tile([P, PASSES, 2, P], F32, tag="bank")
                for g in range(PASSES):
                    for u in range(2):
                        nc.tensor.transpose(
                            flipped[:, g, u, :],
                            pairs[:, (K_PASS // 2) * g + u : (K_PASS // 2) * (g + 1) : 2],
                            identity[:],
                        )
                leave_psum(
                    i % 2 == 1,
                    x_grouped[:, i, :, :].bitcast(F32).rearrange("p g (c u) -> p g c u", u=2),
                    flipped[:].rearrange("p g u c -> p g c u"),
                )
                if i > BLOCKS * b:
                    quantise_x(i - 1)
            quantise_x(BLOCKS * (b + 1) - 1)

        def multiply_weights(bank, words_sb, planes_sb, i, h, t):
            cols = slice(K_PASS * h + P * t, K_PASS * h + P * (t + 1))
            for g in range(PASSES):
                nc.tensor.matmul_mx(
                    out=bank[:, t, :],
                    lhsT=words_sb[:, g, cols].bitcast(FP8X4),
                    lhsT_scale=planes_sb[:, g, cols],
                    rhs=x_words[:, i, g, :].bitcast(FP8X4),
                    rhs_scale=x_scales[:, i, g, :],
                    start=(g == 0),
                    stop=(g == PASSES - 1),
                )

        def project(words_sb, planes_sb, i, h, on_vector, grouped_ap):
            bank = bank_pool.tile([P, PACK, P], F32, tag="bank")
            for t in range(PACK):
                multiply_weights(bank, words_sb, planes_sb, i, h, t)
            leave_psum(on_vector, grouped_ap, bank[:].rearrange("p t c -> p c t"))

        def project_first_keys():
            pair = (0, 1)
            banks = {}
            for j in pair:
                banks[j] = bank_pool.tile([P, PACK, P], F32, tag="bank", name="first_bank")
            for t in range(PACK):
                for j in pair:
                    multiply_weights(banks[j], wk_sb, wk_planes, j, 0, t)
            for j in pair:
                leave_psum(j % 2 == 1, k_grouped[:, 0, 0, P * j : P * (j + 1), :], banks[j][:].rearrange("p t c -> p c t"))

        def project_keys(b, h, j, on_vector):
            project(wk_sb, wk_planes, BLOCKS * b + j, h, on_vector, k_grouped[:, b, h, P * j : P * (j + 1), :])

        def quantise_keys(b, h):
            nc.vector.quantize_mx(
                out=k_words[:, b, h, :].bitcast(FP8X4),
                scales=k_scales[:, b, h, :],
                in_=k_grouped[:, b, h, :, :].rearrange("p c t -> p (c t)"),
            )

        def project_queries(i):
            for h in range(PASSES):
                project(wq_sb, wq_planes, i, h, False, q_grouped[:, i, h, :, :])

        def quantise_queries(i):
            for h in range(PASSES):
                nc.vector.quantize_mx(
                    out=q_words[:, i, h, :].bitcast(FP8X4),
                    scales=q_scales[:, i, h, :],
                    in_=q_grouped[:, i, h, :, :].rearrange("p c t -> p (c t)"),
                )

        scores = {}

        def multiply_scores(i):
            b = i // BLOCKS
            scores[i] = score_pool.tile([P, TOKENS], F32, name="score_bank")
            for h in range(PASSES):
                nc.tensor.matmul_mx(
                    out=scores[i][:],
                    lhsT=q_words[:, i, h, :].bitcast(FP8X4),
                    lhsT_scale=q_scales[:, i, h, :],
                    rhs=k_words[:, b, h, :].bitcast(FP8X4),
                    rhs_scale=k_scales[:, b, h, :],
                    start=(h == 0),
                    stop=(h == PASSES - 1),
                )

        def maxima(i):
            nc.vector.tensor_scalar(out=scaled[:, i, :], in0=scores[i][:], scalar1=-INV_DIVISOR, scalar2=None,
                                    op0=MULT, op1=MIN, accum_out=exp_bias[:, i : i + 1])

        def exponentials(i):
            nc.scalar.activation(out=probs[:, i, :], in_=scaled[:, i, :], func=EXP,
                                 bias=exp_bias[:, i : i + 1], scale=-1.0,
                                 accum_out=row_sum[:, i : i + 1])

        def reciprocals(i):
            nc.vector.reciprocal(out=row_scale[:, i : i + 1], in_=row_sum[:, i : i + 1])

        def scale_and_store(i):
            b, j = divmod(i, BLOCKS)
            rows = out[b, P * j : P * (j + 1), :]
            if i == ALL_BLOCKS - 1:
                for cols in (slice(0, TOKENS // 2), slice(TOKENS // 2, TOKENS)):
                    nc.vector.tensor_scalar_mul(out=probs[:, i, cols], in0=probs[:, i, cols], scalar1=row_scale[:, i : i + 1])
                    nc.sync.dma_start(out=rows[:, cols], in_=probs[:, i, cols])
                return
            if i == ALL_BLOCKS - 3:
                nc.gpsimd.tensor_scalar(out=probs[:, i, :], in0=probs[:, i, :], scalar1=row_scale[:, i : i + 1],
                                        scalar2=0.0, op0=MULT, op1=ADD)
            else:
                nc.vector.tensor_scalar_mul(out=probs[:, i, :], in0=probs[:, i, :], scalar1=row_scale[:, i : i + 1])
            nc.sync.dma_start(out=rows, in_=probs[:, i, :])

        idle_bank = bank_pool.tile([P, TOKENS], F32, tag="bank")
        for _ in range(WARM_UP):
            nc.tensor.matmul(out=idle_bank[:], lhsT=zeros[:, :P], rhs=zeros[:], start=True, stop=True)
        x_to_words(0)
        project_first_keys()
        project_keys(0, 0, 2, False)
        project_keys(0, 0, 3, True)
        quantise_keys(0, 0)
        project_keys(0, 1, 0, False)
        project_keys(0, 1, 1, True)
        project_keys(0, 1, 2, False)
        x_to_words(1)
        project_keys(0, 1, 3, False)
        quantise_keys(0, 1)
        for j in range(BLOCKS):
            project_keys(1, 0, j, j == BLOCKS - 1)
        quantise_keys(1, 0)
        for step in range(ALL_BLOCKS + 3):
            if step >= 3:
                exponentials(step - 3)
            if step < ALL_BLOCKS:
                project_queries(step)
            if 1 <= step <= ALL_BLOCKS:
                quantise_queries(step - 1)
            if 2 <= step <= ALL_BLOCKS + 1:
                maxima(step - 2)
            if step >= 3:
                reciprocals(step - 3)
            if step >= 3:
                scale_and_store(step - 3)
            if 1 <= step <= BLOCKS:
                project_keys(1, 1, step - 1, True)
            if step == BLOCKS:
                quantise_keys(1, 1)
            if 1 <= step <= ALL_BLOCKS:
                multiply_scores(step - 1)
